import numpy as np
import ml_dtypes


def mxq(x, axis, fmt="e4m3"):
    dtype, down = {"e4m3": (ml_dtypes.float8_e4m3fn, 7), "e5m2": (ml_dtypes.float8_e5m2, 14)}[fmt]
    v = np.moveaxis(np.asarray(x, np.float32).astype(ml_dtypes.bfloat16).astype(np.float64), axis, -1)
    blocks = v.reshape(v.shape[:-1] + (-1, 32))
    amax = np.abs(blocks).max(-1, keepdims=True)
    byte = np.maximum(np.where(amax > 0, np.frexp(amax)[1] - 1 + 127, 0) - down, 1)
    scale = np.exp2(byte - 127.0)
    codes = (blocks / scale).astype(np.float32).astype(dtype).astype(np.float64)
    return np.moveaxis((codes * scale).reshape(v.shape), -1, axis)


WIDE = False


def mx_kscale(k):
    if not WIDE:
        return np.ones(k)
    levels = np.array([10, -10, 5, -5, 0])
    if k % 512:
        return np.exp2(np.random.permutation(np.resize(levels, k // 32))).repeat(32)
    a = np.empty((k // 512, 16))
    for p in range(k // 512):
        a[p, :8] = np.random.permutation(np.resize(levels, 8))
        for g in range(8):
            far = levels[np.abs(levels - a[p, g]) >= 10]
            a[p, g + 8] = far[np.random.randint(len(far))]
    return np.exp2(a.ravel()).repeat(32)


BF16 = ml_dtypes.bfloat16


def bf(x):
    return np.asarray(x, np.float32).astype(BF16)


def f64(x):
    return np.asarray(x).astype(np.float64)


N, D, O, H, W = 6, 512, 128, 32, 32
K = D + D
P = H * W


def sigmoid(v):
    return 1.0 / (1.0 + np.exp(-v))


def spatial_gate(re, x_orig):
    a = np.exp(re)
    e = np.exp(a - a.max(1, keepdims=True))
    sm = e / e.sum(1, keepdims=True)
    s = (sm * re).sum(1, keepdims=True)
    return x_orig * s


def setup_inputs():
    t = mx_kscale(D)
    u = t / t.max()
    uc = u[None, :, None, None]
    uu = np.concatenate([u, u])
    return {"x1": bf(np.random.standard_normal((N, D, H, W)) * 0.5 * uc), "x2": bf(np.random.standard_normal((N, D, H, W)) * 0.5 * uc),
            "FE_x1": bf(np.random.standard_normal((N, D, H, W)) * 0.5 * uc), "FE_x2": bf(np.random.standard_normal((N, D, H, W)) * 0.5 * uc),
            "g1": bf(np.random.standard_normal((N, D)) * 1.2), "g2": bf(np.random.standard_normal((N, D)) * 1.2),
            "p1_w": bf(np.random.standard_normal((O, K)) / np.sqrt(K) / uu), "p1_b": bf(np.random.standard_normal(O) * 0.3),
            "p2_w": bf(np.random.standard_normal((O, K)) / np.sqrt(K) / uu), "p2_b": bf(np.random.standard_normal(O) * 0.3)}


def reference(x1, x2, FE_x1, FE_x2, g1, g2, p1_w, p1_b, p2_w, p2_b):
    a1 = f64(x1).reshape(N, D, P)
    a2 = f64(x2).reshape(N, D, P)
    re_x1 = a1 * sigmoid(f64(g1))[:, :, None] + a2
    re_x2 = a2 * sigmoid(f64(g2))[:, :, None] + a1
    fg_x1_sp = spatial_gate(re_x1, a1) + a2
    fg_x2_sp = spatial_gate(re_x2, a2) + a1
    co_x1 = fg_x1_sp + f64(FE_x1).reshape(N, D, P)
    co_x2 = fg_x2_sp + f64(FE_x2).reshape(N, D, P)
    re = np.concatenate([co_x1, co_x2], axis=1)
    rq = mxq(re, 1, "e4m3")
    po_x1 = (mxq(f64(p1_w), 1, "e4m3") @ rq) + f64(p1_b)[None, :, None]
    po_x2 = (mxq(f64(p2_w), 1, "e4m3") @ rq) + f64(p2_b)[None, :, None]
    return po_x1.reshape(N, O, H, W), po_x2.reshape(N, O, H, W)

@@ -1,0 +1,317 @@
+from contextlib import ExitStack
+
+import concourse.mybir as mybir
+from concourse.masks import make_identity
+
+F32 = mybir.dt.float32
+BF16 = mybir.dt.bfloat16
+U32 = mybir.dt.uint32
+U8 = mybir.dt.uint8
+FP8X4 = mybir.dt.float8_e4m3fn_x4
+ALU = mybir.AluOpType
+ACT = mybir.ActivationFunctionType
+
+P = 128
+PACK = 4
+IMAGES = 6
+D = 512
+POS = 1024
+HALF = 512
+BLOCKS = HALF // P
+TWO = 2
+QUARTER = TWO * P
+STREAMS = 2
+PAIRS = IMAGES * (POS // HALF)
+UNITS = PAIRS * STREAMS
+TILES = UNITS * BLOCKS
+OUT = 128
+
+FLOPS = 2 * (2 * OUT) * (STREAMS * D) * (IMAGES * POS)
+
+
+def tile_fr_pb_t_kernel(tc, x1, x2, FE_x1, FE_x2, g1, g2, p1_w, p1_b, p2_w, p2_b, out_0, out_1):
+    nc = tc.nc
+    map_views = [m.rearrange("n (p t) h w -> n p t (h w)", t=PACK) for m in (x1, x2, FE_x1, FE_x2)]
+    out_views = [o.rearrange("n o h w -> n o (h w)") for o in (out_0, out_1)]
+
+    with ExitStack() as ctx:
+        const = ctx.enter_context(tc.tile_pool(name="const", bufs=1))
+        loads = ctx.enter_context(tc.tile_pool(name="loads", bufs=4))
+        wide = ctx.enter_context(tc.tile_pool(name="wide", bufs=3))
+        work = ctx.enter_context(tc.tile_pool(name="work", bufs=2))
+        stats = ctx.enter_context(tc.tile_pool(name="stats", bufs=8))
+        psum = ctx.enter_context(tc.psum_pool(name="psum", bufs=1))
+
+        ident_f32 = const.tile([P, P], F32)
+        make_identity(nc, ident_f32[:])
+        ident_bf16 = const.tile([P, P], BF16)
+        make_identity(nc, ident_bf16[:])
+
+        rows = const.tile([P, D], BF16)
+        nc.vector.memset(rows[:], 0.0)
+        nc.sync.dma_start(out=rows[0:6, :], in_=g1)
+        nc.sync.dma_start(out=rows[6:12, :], in_=g2)
+        nc.sync.dma_start(out=rows[12:13, 0:OUT], in_=p1_b.rearrange("(o p) -> o p", o=1))
+        nc.sync.dma_start(out=rows[13:14, 0:OUT], in_=p2_b.rearrange("(o p) -> o p", o=1))
+
+        maps, scaled_of, other_of, fe_of, grouped_of, codes_of, scales_of, acc_of, result_of = {}, {}, {}, {}, {}, {}, {}, {}, {}
+        rT_of, uT_of, e_of, neg_max_of, sum_e_of, inv_of, s_of = {}, {}, {}, {}, {}, {}, {}
+        xT_of, own_of, coT_of, back_of = {}, {}, {}, {}
+
+        def load_pair(pair):
+            n, half = divmod(pair, POS // HALF)
+            maps[pair] = []
+            for which in range(4):
+                loaded = loads.tile([P, PACK, HALF], BF16, tag="map%d" % which)
+                nc.sync.dma_start(out=loaded[:], in_=map_views[which][n][:, :, half * HALF : (half + 1) * HALF])
+                maps[pair].append(loaded)
+
+        load_pair(0)
+        w_raw = []
+        for w, weight in enumerate((p1_w, p2_w)):
+            raw = const.tile([P, STREAMS * D], BF16, tag="w_raw%d" % w)
+            nc.sync.dma_start(out=raw[:], in_=weight)
+            w_raw.append(raw)
+        load_pair(1)
+
+        columns = psum.tile([P, PACK, P], BF16, tag="xT", bufs=1)
+        for t in range(PACK):
+            nc.tensor.transpose(columns[:, t, :], rows[:, t:D:PACK], ident_bf16[:])
+        gate = const.tile([P, PACK, STREAMS * IMAGES], F32)
+        nc.scalar.activation(out=gate[:], in_=columns[:, :, 0 : STREAMS * IMAGES], func=ACT.Exp, scale=-1.0)
+        nc.vector.tensor_scalar_add(out=gate[:], in0=gate[:], scalar1=1.0)
+        nc.vector.reciprocal(out=gate[:], in_=gate[:])
+        bias_T = psum.tile([P, P], BF16, tag="xT", bufs=1)
+        nc.tensor.transpose(bias_T[:], rows[:, 0:OUT], ident_bf16[:])
+        bias = const.tile([P, 2], F32)
+        nc.vector.tensor_copy(out=bias[:], in_=bias_T[:, 12:14])
+
+        w_grouped = const.tile([P, 2, STREAMS, OUT, PACK], BF16, align_bytes=64)
+        for w in range(2):
+            wT = psum.tile([P, STREAMS, PACK, OUT], BF16, tag="xT", bufs=1)
+            for i in range(STREAMS):
+                for t in range(PACK):
+                    nc.tensor.transpose(wT[:, i, t, :], w_raw[w][:, D * i + t : D * (i + 1) : PACK], ident_bf16[:])
+            nc.vector.tensor_copy(out=w_grouped[:, w], in_=wT[:].rearrange("p i t o -> p i o t"))
+        w_codes = const.tile([P, 2 * STREAMS * OUT], U32, align_bytes=64)
+        w_scales = const.tile([P, 2 * STREAMS * OUT], U8, align_bytes=64)
+        nc.vector.quantize_mx(
+            out=w_codes[:].bitcast(FP8X4),
+            scales=w_scales[:],
+            in_=w_grouped[:].rearrange("p w i o t -> p (w i o t)"),
+        )
+
+        def widen(unit):
+            pair, i = divmod(unit, STREAMS)
+            n = pair // (POS // HALF)
+            scaled = wide.tile([P, PACK, HALF], F32, tag="scaled")
+            for t in range(PACK):
+                nc.gpsimd.tensor_scalar(
+                    out=scaled[:, t, :],
+                    in0=maps[pair][i][:, t, :],
+                    scalar1=gate[:, t, i * IMAGES + n : i * IMAGES + n + 1],
+                    scalar2=0.0,
+                    op0=ALU.mult,
+                    op1=ALU.add,
+                )
+            scaled_of[unit] = scaled
+            other = wide.tile([P, PACK, HALF], F32, tag="other")
+            fe = wide.tile([P, PACK, HALF], F32, tag="fe")
+            for wide_tile, narrow in ((other, maps[pair][1 - i]), (fe, maps[pair][2 + i])):
+                for t in range(0, PACK, 2):
+                    nc.gpsimd.tensor_scalar(
+                        out=wide_tile[:, t : t + 2, :],
+                        in0=narrow[:, t : t + 2, :],
+                        scalar1=1.0,
+                        scalar2=0.0,
+                        op0=ALU.mult,
+                        op1=ALU.add,
+                    )
+            other_of[unit], fe_of[unit] = other, fe
+
+        def place(t):
+            u, e = divmod(t, 2)
+            return slice((2 * e + u) * P, (2 * e + u + 1) * P)
+
+        def add_transposed(out, first, second, b):
+            cols = slice(b * P, (b + 1) * P)
+            for t in range(PACK):
+                part = out[:, place(t)]
+                nc.tensor.matmul(part, lhsT=first[:, t, cols], rhs=ident_f32[:], start=True, stop=False, is_transpose=True)
+                nc.tensor.matmul(part, lhsT=second[:, t, cols], rhs=ident_f32[:], start=False, stop=True, is_transpose=True)
+
+        def transpose_r(t):
+            unit, b = divmod(t, BLOCKS)
+            rT = psum.tile([P, D], F32, tag="rT", bufs=4)
+            add_transposed(rT, scaled_of[unit], other_of[unit], b)
+            rT_of[t] = rT
+
+        def transpose_u(t):
+            unit, b = divmod(t, BLOCKS)
+            uT = psum.tile([P, D], F32, tag="uT", bufs=2)
+            add_transposed(uT, other_of[unit], fe_of[unit], b)
+            uT_of[t] = uT
+
+        def transpose_own(t):
+            xT = psum.tile([P, TWO, D], BF16, tag="xT", bufs=1)
+            for k in range(TWO):
+                unit, b = divmod(t + k, BLOCKS)
+                pair, i = divmod(unit, STREAMS)
+                for j in range(PACK):
+                    nc.tensor.transpose(xT[:, k, place(j)], maps[pair][i][:, j, b * P : (b + 1) * P], ident_bf16[:])
+            xT_of[t] = xT
+
+        def copy_own(t):
+            own = work.tile([P, TWO, D], BF16, tag="own", bufs=3)
+            nc.scalar.copy(out=own[:], in_=xT_of[t][:])
+            own_of[t] = own
+
+        def first_exp(t):
+            e = work.tile([P, D], F32, tag="e", bufs=3)
+            nc.scalar.activation(out=e[:], in_=rT_of[t][:], func=ACT.Exp)
+            e_of[t] = e
+
+        def take_max(t):
+            neg_max = stats.tile([P, 1], F32, tag="neg_max")
+            nc.vector.tensor_reduce(out=neg_max[:], in_=e_of[t][:], axis=mybir.AxisListType.X, op=ALU.max, negate=True)
+            neg_max_of[t] = neg_max
+
+        def second_exp(t):
+            sum_e = stats.tile([P, 1], F32, tag="sum_e")
+            nc.scalar.activation(out=e_of[t][:], in_=e_of[t][:], func=ACT.Exp, bias=neg_max_of[t][:], accum_out=sum_e[:])
+            sum_e_of[t] = sum_e
+
+        def invert_sum(t):
+            inv = stats.tile([P, 1], F32, tag="inv")
+            nc.vector.reciprocal(out=inv[:], in_=sum_e_of[t][:])
+            inv_of[t] = inv
+
+        def weighted_mean(t):
+            s = stats.tile([P, 1], F32, tag="s")
+            nc.vector.scalar_tensor_tensor(
+                out=e_of[t][:],
+                in0=e_of[t][:],
+                scalar=inv_of[t][:],
+                in1=rT_of[t][:],
+                op0=ALU.mult,
+                op1=ALU.mult,
+                accum_out=s[:],
+            )
+            s_of[t] = s
+
+        def fuse(t):
+            order = "q (e w) -> q w e"
+            coT = work.tile([P, D], BF16, tag="coT", bufs=3)
+            nc.vector.scalar_tensor_tensor(
+                out=coT[:].rearrange("q (w e) -> q w e", e=2),
+                in0=own_of[t - t % TWO][:, t % TWO, :].rearrange(order, e=2),
+                scalar=s_of[t][:],
+                in1=uT_of[t][:].rearrange(order, e=2),
+                op0=ALU.mult,
+                op1=ALU.add,
+            )
+            coT_of[t] = coT
+
+        def transpose_back(t):
+            k = t % TWO
+            if k == 0:
+                back = psum.tile([P, 2, TWO * P], F32, tag="back", bufs=1)
+                back_of[t] = back
+            words = coT_of[t][:].bitcast(F32)
+            for u in range(2):
+                nc.tensor.transpose(back_of[t - k][:, u, k * P : (k + 1) * P], words[:, u * P : (u + 1) * P], ident_f32[:])
+
+        def group(t):
+            unit, b = divmod(t, BLOCKS)
+            if b == 0:
+                grouped = work.tile([P, HALF * PACK], BF16, tag="grouped", bufs=2, align_bytes=64)
+                grouped_of[unit] = grouped
+            words = grouped_of[unit][:, b * P * PACK : (b + TWO) * P * PACK].bitcast(F32)
+            nc.scalar.copy(out=words.rearrange("p (w u) -> p w u", u=2), in_=back_of[t][:].rearrange("p u w -> p w u"))
+
+        def quantise(unit):
+            pair, i = divmod(unit, STREAMS)
+            if i == 0:
+                codes = work.tile([P, STREAMS, HALF], U32, tag="codes", bufs=2, align_bytes=64)
+                scales = work.tile([P, STREAMS, HALF], U8, tag="scales", bufs=2, align_bytes=64)
+                codes_of[pair], scales_of[pair] = codes, scales
+            nc.vector.quantize_mx(
+                out=codes_of[pair][:, i, :].bitcast(FP8X4),
+                scales=scales_of[pair][:, i, :],
+                in_=grouped_of[unit][:],
+            )
+
+        def project(pair, quarter):
+            acc = psum.tile([P, 2, QUARTER], F32, tag="rT", bufs=4)
+            q_cols = slice(quarter * QUARTER, (quarter + 1) * QUARTER)
+            for w in range(2):
+                for i in range(STREAMS):
+                    w_cols = slice((w * STREAMS + i) * OUT, (w * STREAMS + i + 1) * OUT)
+                    nc.tensor.matmul_mx(
+                        out=acc[:, w, :],
+                        lhsT=w_codes[:, w_cols].bitcast(FP8X4),
+                        lhsT_scale=w_scales[:, w_cols],
+                        rhs=codes_of[pair][:, i, q_cols].bitcast(FP8X4),
+                        rhs_scale=scales_of[pair][:, i, q_cols],
+                        start=(i == 0),
+                        stop=(i == STREAMS - 1),
+                    )
+            acc_of[(pair, quarter)] = acc
+
+        def store(pair, quarter):
+            n, half = divmod(pair, POS // HALF)
+            if quarter == 0:
+                result = work.tile([P, 2, HALF], F32, tag="result", bufs=2)
+                result_of[pair] = result
+            q_cols = slice(quarter * QUARTER, (quarter + 1) * QUARTER)
+            for w in range(2):
+                nc.scalar.activation(
+                    out=result_of[pair][:, w, q_cols],
+                    in_=acc_of[(pair, quarter)][:, w, :],
+                    func=ACT.Identity,
+                    bias=bias[:, w : w + 1],
+                )
+            if quarter == 1:
+                for w in range(2):
+                    nc.sync.dma_start(out=out_views[w][n, :, half * HALF : (half + 1) * HALF], in_=result_of[pair][:, w, :])
+
+        with tc.manual_schedule():
+            for step in range(-8, TILES + 8):
+                if step >= 0 and step % 8 == 0 and step // 8 + 2 < PAIRS:
+                    load_pair(step // 8 + 2)
+                if step % BLOCKS == 0 and 0 <= step // BLOCKS + 2 < UNITS:
+                    widen(step // BLOCKS + 2)
+
+                if 0 <= step + 1 < TILES:
+                    transpose_r(step + 1)
+                if step % 2 == 1 and 0 <= step + 1 < TILES:
+                    transpose_own(step + 1)
+                if 0 <= step - 1 < TILES:
+                    transpose_u(step - 1)
+
+                if 0 <= step < TILES:
+                    first_exp(step)
+                    take_max(step)
+                if 0 <= step - 1 < TILES:
+                    second_exp(step - 1)
+                    invert_sum(step - 1)
+                if step % 2 == 0 and 0 <= step < TILES:
+                    copy_own(step)
+                if 0 <= step - 2 < TILES:
+                    fuse(step - 2)
+                if step % 2 == 1 and 0 <= step - 5 < TILES:
+                    group(step - 5)
+                if 0 <= step - 3 < TILES:
+                    transpose_back(step - 3)
+                if step % BLOCKS == 0 and 0 <= step // BLOCKS - 2 < UNITS:
+                    quantise(step // BLOCKS - 2)
+                if 0 <= step - 1 < TILES:
+                    weighted_mean(step - 1)
+                if step >= 12 and step % 8 == 4:
+                    project(step // 8 - 1, 0)
+                if step >= 12 and step % 8 == 5:
+                    store(step // 8 - 1, 0)
+                if step >= 12 and step % 8 == 6:
+                    project(step // 8 - 1, 1)
+                if step >= 12 and step % 8 == 7:
+                    store(step // 8 - 1, 1)

@@ -149,6 +149,15 @@ def tile_fr_pb_t_kernel(tc, x1, x2, FE_x1, FE_x2, g1, g2, p1_w, p1_b, p2_w, p2_b
         def transpose_u(t):
             unit, b = divmod(t, BLOCKS)
             uT = psum.tile([P, D], F32, tag="uT", bufs=2)
+            nc.tensor.matmul_mx(
+                out=uT[:],
+                lhsT=w_codes[:, 0:OUT].bitcast(FP8X4),
+                lhsT_scale=w_scales[:, 0:OUT],
+                rhs=w_codes[:].bitcast(FP8X4),
+                rhs_scale=w_scales[:],
+                start=True,
+                stop=True,
+            )
             add_transposed(uT, other_of[unit], fe_of[unit], b)
             uT_of[t] = uT
 

@@ -142,24 +142,26 @@ def tile_fr_pb_t_kernel(tc, x1, x2, FE_x1, FE_x2, g1, g2, p1_w, p1_b, p2_w, p2_b
 
         def transpose_r(t):
             unit, b = divmod(t, BLOCKS)
-            rT = psum.tile([P, D], F32, tag="rT", bufs=4)
+            rT = psum.tile([P, D], F32, tag="rT", bufs=3)
             add_transposed(rT, scaled_of[unit], other_of[unit], b)
             rT_of[t] = rT
 
-        def transpose_u(t):
-            unit, b = divmod(t, BLOCKS)
+        def keep_clock(t, columns):
             uT = psum.tile([P, D], F32, tag="uT", bufs=2)
             nc.tensor.matmul_mx(
-                out=uT[:],
+                out=uT[:, 0:columns],
                 lhsT=w_codes[:, 0:OUT].bitcast(FP8X4),
                 lhsT_scale=w_scales[:, 0:OUT],
-                rhs=w_codes[:].bitcast(FP8X4),
-                rhs_scale=w_scales[:],
+                rhs=w_codes[:, 0:columns].bitcast(FP8X4),
+                rhs_scale=w_scales[:, 0:columns],
                 start=True,
                 stop=True,
             )
-            add_transposed(uT, other_of[unit], fe_of[unit], b)
             uT_of[t] = uT
+
+        def transpose_u(t):
+            unit, b = divmod(t, BLOCKS)
+            add_transposed(uT_of[t], other_of[unit], fe_of[unit], b)
 
         def transpose_own(t):
             xT = psum.tile([P, TWO, D], BF16, tag="xT", bufs=1)
@@ -250,22 +252,22 @@ def tile_fr_pb_t_kernel(tc, x1, x2, FE_x1, FE_x2, g1, g2, p1_w, p1_b, p2_w, p2_b
                 in_=grouped_of[unit][:],
             )
 
-        def project(pair, quarter):
-            acc = psum.tile([P, 2, QUARTER], F32, tag="rT", bufs=4)
+        def project(pair, k, tag="acc", bufs=1):
+            quarter, w, i = k // 4, k // 2 % 2, k % 2
+            if k % 4 == 0:
+                acc = psum.tile([P, 2, QUARTER], F32, tag=tag, bufs=bufs)
+                acc_of[(pair, quarter)] = acc
             q_cols = slice(quarter * QUARTER, (quarter + 1) * QUARTER)
-            for w in range(2):
-                for i in range(STREAMS):
-                    w_cols = slice((w * STREAMS + i) * OUT, (w * STREAMS + i + 1) * OUT)
-                    nc.tensor.matmul_mx(
-                        out=acc[:, w, :],
-                        lhsT=w_codes[:, w_cols].bitcast(FP8X4),
-                        lhsT_scale=w_scales[:, w_cols],
-                        rhs=codes_of[pair][:, i, q_cols].bitcast(FP8X4),
-                        rhs_scale=scales_of[pair][:, i, q_cols],
-                        start=(i == 0),
-                        stop=(i == STREAMS - 1),
-                    )
-            acc_of[(pair, quarter)] = acc
+            w_cols = slice((w * STREAMS + i) * OUT, (w * STREAMS + i + 1) * OUT)
+            nc.tensor.matmul_mx(
+                out=acc_of[(pair, quarter)][:, w, :],
+                lhsT=w_codes[:, w_cols].bitcast(FP8X4),
+                lhsT_scale=w_scales[:, w_cols],
+                rhs=codes_of[pair][:, i, q_cols].bitcast(FP8X4),
+                rhs_scale=scales_of[pair][:, i, q_cols],
+                start=(i == 0),
+                stop=(i == STREAMS - 1),
+            )
 
         def store(pair, quarter):
             n, half = divmod(pair, POS // HALF)
@@ -285,7 +287,7 @@ def tile_fr_pb_t_kernel(tc, x1, x2, FE_x1, FE_x2, g1, g2, p1_w, p1_b, p2_w, p2_b
                     nc.sync.dma_start(out=out_views[w][n, :, half * HALF : (half + 1) * HALF], in_=result_of[pair][:, w, :])
 
         with tc.manual_schedule():
-            for step in range(-8, TILES + 8):
+            for step in range(-8, TILES + 5):
                 if step >= 0 and step % 8 == 0 and step // 8 + 2 < PAIRS:
                     load_pair(step // 8 + 2)
                 if step % BLOCKS == 0 and 0 <= step // BLOCKS + 2 < UNITS:
@@ -295,7 +297,10 @@ def tile_fr_pb_t_kernel(tc, x1, x2, FE_x1, FE_x2, g1, g2, p1_w, p1_b, p2_w, p2_b
                     transpose_r(step + 1)
                 if step % 2 == 1 and 0 <= step + 1 < TILES:
                     transpose_own(step + 1)
+                if step >= 13 and (step - 13) // 8 < PAIRS - 1:
+                    project((step - 13) // 8, (step - 13) % 8)
                 if 0 <= step - 1 < TILES:
+                    keep_clock(step - 1, 512 if step - 1 < 8 else 256)
                     transpose_u(step - 1)
 
                 if 0 <= step < TILES:
@@ -316,11 +321,13 @@ def tile_fr_pb_t_kernel(tc, x1, x2, FE_x1, FE_x2, g1, g2, p1_w, p1_b, p2_w, p2_b
                     quantise(step // BLOCKS - 2)
                 if 0 <= step - 1 < TILES:
                     weighted_mean(step - 1)
-                if step >= 12 and step % 8 == 4:
-                    project(step // 8 - 1, 0)
-                if step >= 12 and step % 8 == 5:
-                    store(step // 8 - 1, 0)
-                if step >= 12 and step % 8 == 6:
-                    project(step // 8 - 1, 1)
-                if step >= 12 and step % 8 == 7:
-                    store(step // 8 - 1, 1)
+                if step >= 16 and (step - 16) // 8 < PAIRS - 1 and step % 4 == 0:
+                    store((step - 16) // 8, step // 4 % 2)
+                if step == TILES + 4:
+                    for k in range(8):
+                        if k < 4:
+                            project(PAIRS - 1, k)
+                        else:
+                            project(PAIRS - 1, k, tag="uT", bufs=2)
+                    store(PAIRS - 1, 0)
+                    store(PAIRS - 1, 1)

@@ -55,7 +55,7 @@ def tile_fr_pb_t_kernel(tc, x1, x2, FE_x1, FE_x2, g1, g2, p1_w, p1_b, p2_w, p2_b
         nc.sync.dma_start(out=rows[13:14, 0:OUT], in_=p2_b.rearrange("(o p) -> o p", o=1))
 
         maps, scaled_of, other_of, fe_of, grouped_of, codes_of, scales_of, acc_of, result_of = {}, {}, {}, {}, {}, {}, {}, {}, {}
-        rT_of, uT_of, e_of, neg_max_of, sum_e_of, inv_of, s_of = {}, {}, {}, {}, {}, {}, {}
+        rT_of, uT_of, e_of, max_r_of, max_a_of, neg_max_of, sum_e_of, inv_of, s_of = {}, {}, {}, {}, {}, {}, {}, {}, {}
         xT_of, own_of, coT_of, back_of = {}, {}, {}, {}
 
         def load_pair(pair):
@@ -101,27 +101,33 @@ def tile_fr_pb_t_kernel(tc, x1, x2, FE_x1, FE_x2, g1, g2, p1_w, p1_b, p2_w, p2_b
             in_=w_grouped[:].rearrange("p w i o t -> p (w i o t)"),
         )
 
-        def widen(unit):
+        def even_odd(positions):
+            return positions.rearrange("p (q m e) -> p q e m", m=P, e=2)
+
+        def scale_gate(unit, t, engine):
             pair, i = divmod(unit, STREAMS)
             n = pair // (POS // HALF)
-            scaled = wide.tile([P, PACK, HALF], F32, tag="scaled")
-            for t in range(PACK):
-                nc.gpsimd.tensor_scalar(
-                    out=scaled[:, t, :],
-                    in0=maps[pair][i][:, t, :],
-                    scalar1=gate[:, t, i * IMAGES + n : i * IMAGES + n + 1],
-                    scalar2=0.0,
-                    op0=ALU.mult,
-                    op1=ALU.add,
-                )
-            scaled_of[unit] = scaled
+            if unit not in scaled_of:
+                scaled = wide.tile([P, PACK, HALF], F32, tag="scaled")
+                scaled_of[unit] = scaled
+            out = scaled_of[unit][:, t, :].rearrange("p (q e m) -> p q e m", e=2, m=P)
+            own = even_odd(maps[pair][i][:, t, :])
+            factor = gate[:, t, i * IMAGES + n : i * IMAGES + n + 1]
+            if engine == "scalar":
+                nc.scalar.activation(out=out, in_=own, func=ACT.Copy, scale=factor)
+            else:
+                nc.gpsimd.tensor_scalar(out=out, in0=own, scalar1=factor, scalar2=0.0, op0=ALU.mult, op1=ALU.add)
+
+        def widen(unit):
+            pair, i = divmod(unit, STREAMS)
             other = wide.tile([P, PACK, HALF], F32, tag="other")
             fe = wide.tile([P, PACK, HALF], F32, tag="fe")
             for wide_tile, narrow in ((other, maps[pair][1 - i]), (fe, maps[pair][2 + i])):
-                for t in range(0, PACK, 2):
+                for q in range(HALF // QUARTER):
+                    cols = slice(q * QUARTER, (q + 1) * QUARTER)
                     nc.gpsimd.tensor_scalar(
-                        out=wide_tile[:, t : t + 2, :],
-                        in0=narrow[:, t : t + 2, :],
+                        out=wide_tile[:, :, cols].rearrange("p t (e m) -> p t e m", e=2),
+                        in0=narrow[:, :, cols].rearrange("p t (m e) -> p t e m", e=2),
                         scalar1=1.0,
                         scalar2=0.0,
                         op0=ALU.mult,
@@ -164,28 +170,38 @@ def tile_fr_pb_t_kernel(tc, x1, x2, FE_x1, FE_x2, g1, g2, p1_w, p1_b, p2_w, p2_b
             add_transposed(uT_of[t], other_of[unit], fe_of[unit], b)
 
         def transpose_own(t):
-            xT = psum.tile([P, TWO, D], BF16, tag="xT", bufs=1)
-            for k in range(TWO):
-                unit, b = divmod(t + k, BLOCKS)
-                pair, i = divmod(unit, STREAMS)
-                for j in range(PACK):
-                    nc.tensor.transpose(xT[:, k, place(j)], maps[pair][i][:, j, b * P : (b + 1) * P], ident_bf16[:])
+            unit, b = divmod(t, BLOCKS)
+            pair, i = divmod(unit, STREAMS)
+            xT = psum.tile([P, D], F32, tag="xT", bufs=1)
+            for j in range(PACK):
+                words = maps[pair][i][:, j, b * P : (b + TWO) * P].bitcast(F32)
+                nc.tensor.transpose(xT[:, place(j)], words, ident_f32[:])
             xT_of[t] = xT
 
         def copy_own(t):
-            own = work.tile([P, TWO, D], BF16, tag="own", bufs=3)
-            nc.scalar.copy(out=own[:], in_=xT_of[t][:])
+            own = work.tile([P, D * TWO], BF16, tag="own", bufs=3)
+            nc.scalar.copy(out=own[:].bitcast(F32), in_=xT_of[t][:])
             own_of[t] = own
+
+        def take_max(t):
+            max_r = stats.tile([P, 1], F32, tag="max_r")
+            nc.vector.tensor_reduce(out=max_r[:], in_=rT_of[t][:], axis=mybir.AxisListType.X, op=ALU.max)
+            max_r_of[t] = max_r
+
+        def exp_max(t):
+            max_a = stats.tile([P, 1], F32, tag="max_a")
+            nc.scalar.activation(out=max_a[:], in_=max_r_of[t][:], func=ACT.Exp)
+            max_a_of[t] = max_a
+
+        def negate(t):
+            neg_max = stats.tile([P, 1], F32, tag="neg_max")
+            nc.vector.tensor_scalar_mul(out=neg_max[:], in0=max_a_of[t][:], scalar1=-1.0)
+            neg_max_of[t] = neg_max
 
         def first_exp(t):
             e = work.tile([P, D], F32, tag="e", bufs=3)
             nc.scalar.activation(out=e[:], in_=rT_of[t][:], func=ACT.Exp)
             e_of[t] = e
-
-        def take_max(t):
-            neg_max = stats.tile([P, 1], F32, tag="neg_max")
-            nc.vector.tensor_reduce(out=neg_max[:], in_=e_of[t][:], axis=mybir.AxisListType.X, op=ALU.max, negate=True)
-            neg_max_of[t] = neg_max
 
         def second_exp(t):
             sum_e = stats.tile([P, 1], F32, tag="sum_e")
@@ -211,13 +227,13 @@ def tile_fr_pb_t_kernel(tc, x1, x2, FE_x1, FE_x2, g1, g2, p1_w, p1_b, p2_w, p2_b
             s_of[t] = s
 
         def fuse(t):
-            order = "q (e w) -> q w e"
+            k = t % TWO
             coT = work.tile([P, D], BF16, tag="coT", bufs=3)
             nc.vector.scalar_tensor_tensor(
                 out=coT[:].rearrange("q (w e) -> q w e", e=2),
-                in0=own_of[t - t % TWO][:, t % TWO, :].rearrange(order, e=2),
+                in0=own_of[t - k][:].rearrange("q (e w k) -> q w e k", e=2, k=TWO)[:, :, :, k],
                 scalar=s_of[t][:],
-                in1=uT_of[t][:].rearrange(order, e=2),
+                in1=uT_of[t][:].rearrange("q (e w) -> q w e", e=2),
                 op0=ALU.mult,
                 op1=ALU.add,
             )
@@ -277,8 +293,8 @@ def tile_fr_pb_t_kernel(tc, x1, x2, FE_x1, FE_x2, g1, g2, p1_w, p1_b, p2_w, p2_b
             q_cols = slice(quarter * QUARTER, (quarter + 1) * QUARTER)
             for w in range(2):
                 nc.scalar.activation(
-                    out=result_of[pair][:, w, q_cols],
-                    in_=acc_of[(pair, quarter)][:, w, :],
+                    out=result_of[pair][:, w, q_cols].rearrange("p (m e) -> p m e", e=2),
+                    in_=acc_of[(pair, quarter)][:, w, :].rearrange("p (e m) -> p m e", e=2),
                     func=ACT.Identity,
                     bias=bias[:, w : w + 1],
                 )
@@ -290,8 +306,14 @@ def tile_fr_pb_t_kernel(tc, x1, x2, FE_x1, FE_x2, g1, g2, p1_w, p1_b, p2_w, p2_b
             for step in range(-8, TILES + 5):
                 if step >= 0 and step % 8 == 0 and step // 8 + 2 < PAIRS:
                     load_pair(step // 8 + 2)
-                if step % BLOCKS == 0 and 0 <= step // BLOCKS + 2 < UNITS:
-                    widen(step // BLOCKS + 2)
+                unit = step // BLOCKS + 2
+                if unit < UNITS:
+                    if step % BLOCKS == 0:
+                        scale_gate(unit, 2, "gpsimd")
+                        scale_gate(unit, 3, "gpsimd")
+                        widen(unit)
+                    elif step % BLOCKS < 3:
+                        scale_gate(unit, step % BLOCKS - 1, "scalar")
 
                 if 0 <= step + 1 < TILES:
                     transpose_r(step + 1)
@@ -304,15 +326,20 @@ def tile_fr_pb_t_kernel(tc, x1, x2, FE_x1, FE_x2, g1, g2, p1_w, p1_b, p2_w, p2_b
                     transpose_u(step - 1)
 
                 if 0 <= step < TILES:
-                    first_exp(step)
                     take_max(step)
                 if 0 <= step - 1 < TILES:
                     second_exp(step - 1)
-                    invert_sum(step - 1)
-                if step % 2 == 0 and 0 <= step < TILES:
-                    copy_own(step)
+                if 0 <= step < TILES:
+                    exp_max(step)
+                    first_exp(step)
                 if 0 <= step - 2 < TILES:
                     fuse(step - 2)
+                if 0 <= step - 1 < TILES:
+                    invert_sum(step - 1)
+                if 0 <= step < TILES:
+                    negate(step)
+                if step % 2 == 0 and 0 <= step < TILES:
+                    copy_own(step)
                 if step % 2 == 1 and 0 <= step - 5 < TILES:
                     group(step - 5)
                 if 0 <= step - 3 < TILES:

@@ -55,7 +55,7 @@ def tile_fr_pb_t_kernel(tc, x1, x2, FE_x1, FE_x2, g1, g2, p1_w, p1_b, p2_w, p2_b
         nc.sync.dma_start(out=rows[13:14, 0:OUT], in_=p2_b.rearrange("(o p) -> o p", o=1))
 
         maps, scaled_of, other_of, fe_of, grouped_of, codes_of, scales_of, acc_of, result_of = {}, {}, {}, {}, {}, {}, {}, {}, {}
-        rT_of, uT_of, e_of, max_r_of, max_a_of, neg_max_of, sum_e_of, inv_of, s_of = {}, {}, {}, {}, {}, {}, {}, {}, {}
+        rT_of, uT_of, e_of, neg_max_of, sum_e_of, inv_of, s_of = {}, {}, {}, {}, {}, {}, {}
         xT_of, own_of, coT_of, back_of = {}, {}, {}, {}
 
         def load_pair(pair):
@@ -104,7 +104,7 @@ def tile_fr_pb_t_kernel(tc, x1, x2, FE_x1, FE_x2, g1, g2, p1_w, p1_b, p2_w, p2_b
         def even_odd(positions):
             return positions.rearrange("p (q m e) -> p q e m", m=P, e=2)
 
-        def scale_gate(unit, t, engine):
+        def scale_gate(unit, t):
             pair, i = divmod(unit, STREAMS)
             n = pair // (POS // HALF)
             if unit not in scaled_of:
@@ -113,7 +113,7 @@ def tile_fr_pb_t_kernel(tc, x1, x2, FE_x1, FE_x2, g1, g2, p1_w, p1_b, p2_w, p2_b
             out = scaled_of[unit][:, t, :].rearrange("p (q e m) -> p q e m", e=2, m=P)
             own = even_odd(maps[pair][i][:, t, :])
             factor = gate[:, t, i * IMAGES + n : i * IMAGES + n + 1]
-            if engine == "scalar":
+            if t == 3:
                 nc.scalar.activation(out=out, in_=own, func=ACT.Copy, scale=factor)
             else:
                 nc.gpsimd.tensor_scalar(out=out, in0=own, scalar1=factor, scalar2=0.0, op0=ALU.mult, op1=ALU.add)
@@ -152,14 +152,14 @@ def tile_fr_pb_t_kernel(tc, x1, x2, FE_x1, FE_x2, g1, g2, p1_w, p1_b, p2_w, p2_b
             add_transposed(rT, scaled_of[unit], other_of[unit], b)
             rT_of[t] = rT
 
-        def keep_clock(t, columns):
+        def keep_clock(t):
             uT = psum.tile([P, D], F32, tag="uT", bufs=2)
             nc.tensor.matmul_mx(
-                out=uT[:, 0:columns],
+                out=uT[:],
                 lhsT=w_codes[:, 0:OUT].bitcast(FP8X4),
                 lhsT_scale=w_scales[:, 0:OUT],
-                rhs=w_codes[:, 0:columns].bitcast(FP8X4),
-                rhs_scale=w_scales[:, 0:columns],
+                rhs=w_codes[:].bitcast(FP8X4),
+                rhs_scale=w_scales[:],
                 start=True,
                 stop=True,
             )
@@ -180,22 +180,13 @@ def tile_fr_pb_t_kernel(tc, x1, x2, FE_x1, FE_x2, g1, g2, p1_w, p1_b, p2_w, p2_b
 
         def copy_own(t):
             own = work.tile([P, D * TWO], BF16, tag="own", bufs=3)
-            nc.scalar.copy(out=own[:].bitcast(F32), in_=xT_of[t][:])
+            words = own[:].bitcast(F32).rearrange("q (w e) -> q w e", e=2)
+            nc.scalar.copy(out=words, in_=xT_of[t][:].rearrange("q (e w) -> q w e", e=2))
             own_of[t] = own
 
         def take_max(t):
-            max_r = stats.tile([P, 1], F32, tag="max_r")
-            nc.vector.tensor_reduce(out=max_r[:], in_=rT_of[t][:], axis=mybir.AxisListType.X, op=ALU.max)
-            max_r_of[t] = max_r
-
-        def exp_max(t):
-            max_a = stats.tile([P, 1], F32, tag="max_a")
-            nc.scalar.activation(out=max_a[:], in_=max_r_of[t][:], func=ACT.Exp)
-            max_a_of[t] = max_a
-
-        def negate(t):
             neg_max = stats.tile([P, 1], F32, tag="neg_max")
-            nc.vector.tensor_scalar_mul(out=neg_max[:], in0=max_a_of[t][:], scalar1=-1.0)
+            nc.vector.tensor_reduce(out=neg_max[:], in_=e_of[t][:], axis=mybir.AxisListType.X, op=ALU.max, negate=True)
             neg_max_of[t] = neg_max
 
         def first_exp(t):
@@ -231,7 +222,7 @@ def tile_fr_pb_t_kernel(tc, x1, x2, FE_x1, FE_x2, g1, g2, p1_w, p1_b, p2_w, p2_b
             coT = work.tile([P, D], BF16, tag="coT", bufs=3)
             nc.vector.scalar_tensor_tensor(
                 out=coT[:].rearrange("q (w e) -> q w e", e=2),
-                in0=own_of[t - k][:].rearrange("q (e w k) -> q w e k", e=2, k=TWO)[:, :, :, k],
+                in0=own_of[t - k][:].rearrange("q (w e k) -> q w e k", e=2, k=TWO)[:, :, :, k],
                 scalar=s_of[t][:],
                 in1=uT_of[t][:].rearrange("q (e w) -> q w e", e=2),
                 op0=ALU.mult,
@@ -309,11 +300,11 @@ def tile_fr_pb_t_kernel(tc, x1, x2, FE_x1, FE_x2, g1, g2, p1_w, p1_b, p2_w, p2_b
                 unit = step // BLOCKS + 2
                 if unit < UNITS:
                     if step % BLOCKS == 0:
-                        scale_gate(unit, 2, "gpsimd")
-                        scale_gate(unit, 3, "gpsimd")
+                        for t in range(3):
+                            scale_gate(unit, t)
                         widen(unit)
-                    elif step % BLOCKS < 3:
-                        scale_gate(unit, step % BLOCKS - 1, "scalar")
+                    elif step % BLOCKS == 2:
+                        scale_gate(unit, 3)
 
                 if 0 <= step + 1 < TILES:
                     transpose_r(step + 1)
@@ -322,32 +313,29 @@ def tile_fr_pb_t_kernel(tc, x1, x2, FE_x1, FE_x2, g1, g2, p1_w, p1_b, p2_w, p2_b
                 if step >= 13 and (step - 13) // 8 < PAIRS - 1:
                     project((step - 13) // 8, (step - 13) % 8)
                 if 0 <= step - 1 < TILES:
-                    keep_clock(step - 1, 512 if step - 1 < 8 else 256)
+                    keep_clock(step - 1)
                     transpose_u(step - 1)
 
+                if 0 <= step - 1 < TILES:
+                    second_exp(step - 1)
+                if step % 2 == 1 and 0 <= step - 5 < TILES:
+                    group(step - 5)
+                if step % 2 == 0 and 0 <= step < TILES:
+                    copy_own(step)
                 if 0 <= step < TILES:
                     take_max(step)
                 if 0 <= step - 1 < TILES:
-                    second_exp(step - 1)
-                if 0 <= step < TILES:
-                    exp_max(step)
-                    first_exp(step)
+                    invert_sum(step - 1)
                 if 0 <= step - 2 < TILES:
                     fuse(step - 2)
-                if 0 <= step - 1 < TILES:
-                    invert_sum(step - 1)
-                if 0 <= step < TILES:
-                    negate(step)
-                if step % 2 == 0 and 0 <= step < TILES:
-                    copy_own(step)
-                if step % 2 == 1 and 0 <= step - 5 < TILES:
-                    group(step - 5)
-                if 0 <= step - 3 < TILES:
-                    transpose_back(step - 3)
                 if step % BLOCKS == 0 and 0 <= step // BLOCKS - 2 < UNITS:
                     quantise(step // BLOCKS - 2)
+                if 0 <= step - 3 < TILES:
+                    transpose_back(step - 3)
                 if 0 <= step - 1 < TILES:
                     weighted_mean(step - 1)
+                if 0 <= step + 1 < TILES:
+                    first_exp(step + 1)
                 if step >= 16 and (step - 16) // 8 < PAIRS - 1 and step % 4 == 0:
                     store((step - 16) // 8, step // 4 % 2)
                 if step == TILES + 4:

@@ -141,10 +141,16 @@ def tile_fr_pb_t_kernel(tc, x1, x2, FE_x1, FE_x2, g1, g2, p1_w, p1_b, p2_w, p2_b
 
         def add_transposed(out, first, second, b):
             cols = slice(b * P, (b + 1) * P)
-            for t in range(PACK):
-                part = out[:, place(t)]
-                nc.tensor.matmul(part, lhsT=first[:, t, cols], rhs=ident_f32[:], start=True, stop=False, is_transpose=True)
-                nc.tensor.matmul(part, lhsT=second[:, t, cols], rhs=ident_f32[:], start=False, stop=True, is_transpose=True)
+            for k, source in enumerate((first, second)):
+                for t in range(PACK):
+                    nc.tensor.matmul(
+                        out[:, place(t)],
+                        lhsT=source[:, t, cols],
+                        rhs=ident_f32[:],
+                        start=(k == 0 and t == 0),
+                        stop=(k == 1 and t == PACK - 1),
+                        is_transpose=True,
+                    )
 
         def transpose_r(t):
             unit, b = divmod(t, BLOCKS)

@@ -55,23 +55,28 @@ def tile_fr_pb_t_kernel(tc, x1, x2, FE_x1, FE_x2, g1, g2, p1_w, p1_b, p2_w, p2_b
         nc.sync.dma_start(out=rows[13:14, 0:OUT], in_=p2_b.rearrange("(o p) -> o p", o=1))
 
         maps, scaled_of, other_of, fe_of, grouped_of, codes_of, scales_of, acc_of, result_of = {}, {}, {}, {}, {}, {}, {}, {}, {}
-        rT_of, uT_of, e_of, neg_max_of, sum_e_of, inv_of, s_of = {}, {}, {}, {}, {}, {}, {}
+        rT_of, uT_of, e_of, max_r_of, max_a_of, neg_max_of, sum_e_of, inv_of, s_of = {}, {}, {}, {}, {}, {}, {}, {}, {}
         xT_of, own_of, coT_of, back_of = {}, {}, {}, {}
 
-        def load_pair(pair):
+        def load_map(pair, which):
             n, half = divmod(pair, POS // HALF)
-            maps[pair] = []
-            for which in range(4):
-                loaded = loads.tile([P, PACK, HALF], BF16, tag="map%d" % which)
-                nc.sync.dma_start(out=loaded[:], in_=map_views[which][n][:, :, half * HALF : (half + 1) * HALF])
-                maps[pair].append(loaded)
+            loaded = loads.tile([P, PACK, HALF], BF16, tag="map%d" % which)
+            nc.sync.dma_start(out=loaded[:], in_=map_views[which][n][:, :, half * HALF : (half + 1) * HALF])
+            maps.setdefault(pair, {})[which] = loaded
 
-        load_pair(0)
+        def load_pair(pair):
+            for which in range(4):
+                load_map(pair, which)
+
+        load_map(0, 1)
+        load_map(0, 0)
         w_raw = []
         for w, weight in enumerate((p1_w, p2_w)):
             raw = const.tile([P, STREAMS * D], BF16, tag="w_raw%d" % w)
             nc.sync.dma_start(out=raw[:], in_=weight)
             w_raw.append(raw)
+        load_map(0, 2)
+        load_map(0, 3)
         load_pair(1)
 
         columns = psum.tile([P, PACK, P], BF16, tag="xT", bufs=1)
@@ -104,7 +109,7 @@ def tile_fr_pb_t_kernel(tc, x1, x2, FE_x1, FE_x2, g1, g2, p1_w, p1_b, p2_w, p2_b
         def even_odd(positions):
             return positions.rearrange("p (q m e) -> p q e m", m=P, e=2)
 
-        def scale_gate(unit, t):
+        def scale_gate(unit, t, engine):
             pair, i = divmod(unit, STREAMS)
             n = pair // (POS // HALF)
             if unit not in scaled_of:
@@ -113,8 +118,10 @@ def tile_fr_pb_t_kernel(tc, x1, x2, FE_x1, FE_x2, g1, g2, p1_w, p1_b, p2_w, p2_b
             out = scaled_of[unit][:, t, :].rearrange("p (q e m) -> p q e m", e=2, m=P)
             own = even_odd(maps[pair][i][:, t, :])
             factor = gate[:, t, i * IMAGES + n : i * IMAGES + n + 1]
-            if t == 3:
+            if engine == "scalar":
                 nc.scalar.activation(out=out, in_=own, func=ACT.Copy, scale=factor)
+            elif engine == "vector":
+                nc.vector.tensor_scalar_mul(out=out, in0=own, scalar1=factor)
             else:
                 nc.gpsimd.tensor_scalar(out=out, in0=own, scalar1=factor, scalar2=0.0, op0=ALU.mult, op1=ALU.add)
 
@@ -191,8 +198,18 @@ def tile_fr_pb_t_kernel(tc, x1, x2, FE_x1, FE_x2, g1, g2, p1_w, p1_b, p2_w, p2_b
             own_of[t] = own
 
         def take_max(t):
+            max_r = stats.tile([P, 1], F32, tag="max_r")
+            nc.vector.tensor_reduce(out=max_r[:], in_=rT_of[t][:], axis=mybir.AxisListType.X, op=ALU.max)
+            max_r_of[t] = max_r
+
+        def exp_max(t):
+            max_a = stats.tile([P, 1], F32, tag="max_a")
+            nc.scalar.activation(out=max_a[:], in_=max_r_of[t][:], func=ACT.Exp)
+            max_a_of[t] = max_a
+
+        def negate(t):
             neg_max = stats.tile([P, 1], F32, tag="neg_max")
-            nc.vector.tensor_reduce(out=neg_max[:], in_=e_of[t][:], axis=mybir.AxisListType.X, op=ALU.max, negate=True)
+            nc.vector.tensor_scalar_mul(out=neg_max[:], in0=max_a_of[t][:], scalar1=-1.0)
             neg_max_of[t] = neg_max
 
         def first_exp(t):
@@ -253,16 +270,16 @@ def tile_fr_pb_t_kernel(tc, x1, x2, FE_x1, FE_x2, g1, g2, p1_w, p1_b, p2_w, p2_b
             words = grouped_of[unit][:, b * P * PACK : (b + TWO) * P * PACK].bitcast(F32)
             nc.scalar.copy(out=words.rearrange("p (w u) -> p w u", u=2), in_=back_of[t][:].rearrange("p u w -> p w u"))
 
-        def quantise(unit):
+        def quantise(unit, first=0, columns=HALF):
             pair, i = divmod(unit, STREAMS)
             if i == 0:
                 codes = work.tile([P, STREAMS, HALF], U32, tag="codes", bufs=2, align_bytes=64)
                 scales = work.tile([P, STREAMS, HALF], U8, tag="scales", bufs=2, align_bytes=64)
                 codes_of[pair], scales_of[pair] = codes, scales
             nc.vector.quantize_mx(
-                out=codes_of[pair][:, i, :].bitcast(FP8X4),
-                scales=scales_of[pair][:, i, :],
-                in_=grouped_of[unit][:],
+                out=codes_of[pair][:, i, first : first + columns].bitcast(FP8X4),
+                scales=scales_of[pair][:, i, first : first + columns],
+                in_=grouped_of[unit][:, first * PACK : (first + columns) * PACK],
             )
 
         def project(pair, k, tag="acc", bufs=1):
@@ -295,22 +312,34 @@ def tile_fr_pb_t_kernel(tc, x1, x2, FE_x1, FE_x2, g1, g2, p1_w, p1_b, p2_w, p2_b
                     func=ACT.Identity,
                     bias=bias[:, w : w + 1],
                 )
-            if quarter == 1:
-                for w in range(2):
-                    nc.sync.dma_start(out=out_views[w][n, :, half * HALF : (half + 1) * HALF], in_=result_of[pair][:, w, :])
+            if pair == PAIRS - 1:
+                stored = q_cols
+            elif quarter == 1:
+                stored = slice(0, HALF)
+            else:
+                return
+            for w in range(2):
+                nc.sync.dma_start(
+                    out=out_views[w][n, :, half * HALF + stored.start : half * HALF + stored.stop],
+                    in_=result_of[pair][:, w, stored],
+                )
 
         with tc.manual_schedule():
             for step in range(-8, TILES + 5):
                 if step >= 0 and step % 8 == 0 and step // 8 + 2 < PAIRS:
                     load_pair(step // 8 + 2)
                 unit = step // BLOCKS + 2
-                if unit < UNITS:
+                if unit == 0:
+                    if step % BLOCKS == 0:
+                        widen(unit)
+                        for t in range(2):
+                            scale_gate(unit, t, "vector")
+                            scale_gate(unit, t + 2, "scalar")
+                elif unit < UNITS:
                     if step % BLOCKS == 0:
                         for t in range(3):
-                            scale_gate(unit, t)
+                            scale_gate(unit, t, "gpsimd")
                         widen(unit)
-                    elif step % BLOCKS == 2:
-                        scale_gate(unit, 3)
 
                 if 0 <= step + 1 < TILES:
                     transpose_r(step + 1)
@@ -323,32 +352,36 @@ def tile_fr_pb_t_kernel(tc, x1, x2, FE_x1, FE_x2, g1, g2, p1_w, p1_b, p2_w, p2_b
                     transpose_u(step - 1)
 
                 if 0 <= step - 1 < TILES:
-                    second_exp(step - 1)
+                    invert_sum(step - 1)
                 if step % 2 == 1 and 0 <= step - 5 < TILES:
                     group(step - 5)
                 if step % 2 == 0 and 0 <= step < TILES:
                     copy_own(step)
                 if 0 <= step < TILES:
-                    take_max(step)
-                if 0 <= step - 1 < TILES:
-                    invert_sum(step - 1)
+                    exp_max(step)
+                    first_exp(step)
+                if step % BLOCKS == 2 and 1 <= unit < UNITS:
+                    scale_gate(unit, 3, "scalar")
                 if 0 <= step - 2 < TILES:
                     fuse(step - 2)
-                if step % BLOCKS == 0 and 0 <= step // BLOCKS - 2 < UNITS:
-                    quantise(step // BLOCKS - 2)
+                if 0 <= step < TILES:
+                    negate(step)
                 if 0 <= step - 3 < TILES:
                     transpose_back(step - 3)
+                if step % BLOCKS == 0 and 0 <= step // BLOCKS - 2 < UNITS - 1:
+                    quantise(step // BLOCKS - 2)
+                if step in (TILES + 2, TILES + 4):
+                    quantise(UNITS - 1, (step - TILES - 2) // 2 * QUARTER, QUARTER)
                 if 0 <= step - 1 < TILES:
                     weighted_mean(step - 1)
                 if 0 <= step + 1 < TILES:
-                    first_exp(step + 1)
+                    take_max(step + 1)
+                if 0 <= step < TILES:
+                    second_exp(step)
                 if step >= 16 and (step - 16) // 8 < PAIRS - 1 and step % 4 == 0:
                     store((step - 16) // 8, step // 4 % 2)
-                if step == TILES + 4:
-                    for k in range(8):
-                        if k < 4:
-                            project(PAIRS - 1, k)
-                        else:
-                            project(PAIRS - 1, k, tag="uT", bufs=2)
-                    store(PAIRS - 1, 0)
-                    store(PAIRS - 1, 1)
+                if step in (TILES + 2, TILES + 4):
+                    quarter = (step - TILES - 2) // 2
+                    for k in range(4):
+                        project(PAIRS - 1, 4 * quarter + k, tag="uT", bufs=2)
+                    store(PAIRS - 1, quarter)

from contextlib import ExitStack

import concourse.mybir as mybir
from concourse.masks import make_identity

F32 = mybir.dt.float32
BF16 = mybir.dt.bfloat16
U32 = mybir.dt.uint32
U8 = mybir.dt.uint8
FP8X4 = mybir.dt.float8_e4m3fn_x4
ALU = mybir.AluOpType
ACT = mybir.ActivationFunctionType

P = 128
PACK = 4
IMAGES = 6
D = 512
POS = 1024
HALF = 512
BLOCKS = HALF // P
TWO = 2
QUARTER = TWO * P
STREAMS = 2
PAIRS = IMAGES * (POS // HALF)
UNITS = PAIRS * STREAMS
TILES = UNITS * BLOCKS
OUT = 128

FLOPS = 2 * (2 * OUT) * (STREAMS * D) * (IMAGES * POS)


def tile_fr_pb_t_kernel(tc, x1, x2, FE_x1, FE_x2, g1, g2, p1_w, p1_b, p2_w, p2_b, out_0, out_1):
    nc = tc.nc
    map_views = [m.rearrange("n (p t) h w -> n p t (h w)", t=PACK) for m in (x1, x2, FE_x1, FE_x2)]
    out_views = [o.rearrange("n o h w -> n o (h w)") for o in (out_0, out_1)]

    with ExitStack() as ctx:
        const = ctx.enter_context(tc.tile_pool(name="const", bufs=1))
        loads = ctx.enter_context(tc.tile_pool(name="loads", bufs=4))
        wide = ctx.enter_context(tc.tile_pool(name="wide", bufs=3))
        work = ctx.enter_context(tc.tile_pool(name="work", bufs=2))
        stats = ctx.enter_context(tc.tile_pool(name="stats", bufs=8))
        psum = ctx.enter_context(tc.psum_pool(name="psum", bufs=1))

        ident_f32 = const.tile([P, P], F32)
        make_identity(nc, ident_f32[:])
        ident_bf16 = const.tile([P, P], BF16)
        make_identity(nc, ident_bf16[:])

        rows = const.tile([P, D], BF16)
        nc.vector.memset(rows[:], 0.0)
        nc.sync.dma_start(out=rows[0:6, :], in_=g1)
        nc.sync.dma_start(out=rows[6:12, :], in_=g2)
        nc.sync.dma_start(out=rows[12:13, 0:OUT], in_=p1_b.rearrange("(o p) -> o p", o=1))
        nc.sync.dma_start(out=rows[13:14, 0:OUT], in_=p2_b.rearrange("(o p) -> o p", o=1))

        maps, scaled_of, other_of, fe_of, grouped_of, codes_of, scales_of, acc_of, result_of = {}, {}, {}, {}, {}, {}, {}, {}, {}
        rT_of, uT_of, e_of, max_r_of, max_a_of, neg_max_of, sum_e_of, inv_of, s_of = {}, {}, {}, {}, {}, {}, {}, {}, {}
        xT_of, own_of, coT_of, back_of = {}, {}, {}, {}

        def load_map(pair, which):
            n, half = divmod(pair, POS // HALF)
            loaded = loads.tile([P, PACK, HALF], BF16, tag="map%d" % which)
            nc.sync.dma_start(out=loaded[:], in_=map_views[which][n][:, :, half * HALF : (half + 1) * HALF])
            maps.setdefault(pair, {})[which] = loaded

        def load_pair(pair):
            for which in range(4):
                load_map(pair, which)

        load_map(0, 1)
        load_map(0, 0)
        w_raw = []
        for w, weight in enumerate((p1_w, p2_w)):
            raw = const.tile([P, STREAMS * D], BF16, tag="w_raw%d" % w)
            nc.sync.dma_start(out=raw[:], in_=weight)
            w_raw.append(raw)
        load_map(0, 2)
        load_map(0, 3)
        load_pair(1)

        columns = psum.tile([P, PACK, P], BF16, tag="xT", bufs=1)
        for t in range(PACK):
            nc.tensor.transpose(columns[:, t, :], rows[:, t:D:PACK], ident_bf16[:])
        gate = const.tile([P, PACK, STREAMS * IMAGES], F32)
        nc.scalar.activation(out=gate[:], in_=columns[:, :, 0 : STREAMS * IMAGES], func=ACT.Exp, scale=-1.0)
        nc.vector.tensor_scalar_add(out=gate[:], in0=gate[:], scalar1=1.0)
        nc.vector.reciprocal(out=gate[:], in_=gate[:])
        bias_T = psum.tile([P, P], BF16, tag="xT", bufs=1)
        nc.tensor.transpose(bias_T[:], rows[:, 0:OUT], ident_bf16[:])
        bias = const.tile([P, 2], F32)
        nc.vector.tensor_copy(out=bias[:], in_=bias_T[:, 12:14])

        w_grouped = const.tile([P, 2, STREAMS, OUT, PACK], BF16, align_bytes=64)
        for w in range(2):
            wT = psum.tile([P, STREAMS, PACK, OUT], BF16, tag="xT", bufs=1)
            for i in range(STREAMS):
                for t in range(PACK):
                    nc.tensor.transpose(wT[:, i, t, :], w_raw[w][:, D * i + t : D * (i + 1) : PACK], ident_bf16[:])
            nc.vector.tensor_copy(out=w_grouped[:, w], in_=wT[:].rearrange("p i t o -> p i o t"))
        w_codes = const.tile([P, 2 * STREAMS * OUT], U32, align_bytes=64)
        w_scales = const.tile([P, 2 * STREAMS * OUT], U8, align_bytes=64)
        nc.vector.quantize_mx(
            out=w_codes[:].bitcast(FP8X4),
            scales=w_scales[:],
            in_=w_grouped[:].rearrange("p w i o t -> p (w i o t)"),
        )

        def even_odd(positions):
            return positions.rearrange("p (q m e) -> p q e m", m=P, e=2)

        def scale_gate(unit, t, engine):
            pair, i = divmod(unit, STREAMS)
            n = pair // (POS // HALF)
            if unit not in scaled_of:
                scaled = wide.tile([P, PACK, HALF], F32, tag="scaled")
                scaled_of[unit] = scaled
            out = scaled_of[unit][:, t, :].rearrange("p (q e m) -> p q e m", e=2, m=P)
            own = even_odd(maps[pair][i][:, t, :])
            factor = gate[:, t, i * IMAGES + n : i * IMAGES + n + 1]
            if engine == "scalar":
                nc.scalar.activation(out=out, in_=own, func=ACT.Copy, scale=factor)
            elif engine == "vector":
                nc.vector.tensor_scalar_mul(out=out, in0=own, scalar1=factor)
            else:
                nc.gpsimd.tensor_scalar(out=out, in0=own, scalar1=factor, scalar2=0.0, op0=ALU.mult, op1=ALU.add)

        def widen(unit):
            pair, i = divmod(unit, STREAMS)
            other = wide.tile([P, PACK, HALF], F32, tag="other")
            fe = wide.tile([P, PACK, HALF], F32, tag="fe")
            for wide_tile, narrow in ((other, maps[pair][1 - i]), (fe, maps[pair][2 + i])):
                for q in range(HALF // QUARTER):
                    cols = slice(q * QUARTER, (q + 1) * QUARTER)
                    nc.gpsimd.tensor_scalar(
                        out=wide_tile[:, :, cols].rearrange("p t (e m) -> p t e m", e=2),
                        in0=narrow[:, :, cols].rearrange("p t (m e) -> p t e m", e=2),
                        scalar1=1.0,
                        scalar2=0.0,
                        op0=ALU.mult,
                        op1=ALU.add,
                    )
            other_of[unit], fe_of[unit] = other, fe

        def place(t):
            u, e = divmod(t, 2)
            return slice((2 * e + u) * P, (2 * e + u + 1) * P)

        def add_transposed(out, first, second, b):
            cols = slice(b * P, (b + 1) * P)
            for k, source in enumerate((first, second)):
                for t in range(PACK):
                    nc.tensor.matmul(
                        out[:, place(t)],
                        lhsT=source[:, t, cols],
                        rhs=ident_f32[:],
                        start=(k == 0 and t == 0),
                        stop=(k == 1 and t == PACK - 1),
                        is_transpose=True,
                    )

        def transpose_r(t):
            unit, b = divmod(t, BLOCKS)
            rT = psum.tile([P, D], F32, tag="rT", bufs=3)
            add_transposed(rT, scaled_of[unit], other_of[unit], b)
            rT_of[t] = rT

        def keep_clock(t):
            uT = psum.tile([P, D], F32, tag="uT", bufs=2)
            nc.tensor.matmul_mx(
                out=uT[:],
                lhsT=w_codes[:, 0:OUT].bitcast(FP8X4),
                lhsT_scale=w_scales[:, 0:OUT],
                rhs=w_codes[:].bitcast(FP8X4),
                rhs_scale=w_scales[:],
                start=True,
                stop=True,
            )
            uT_of[t] = uT

        def transpose_u(t):
            unit, b = divmod(t, BLOCKS)
            add_transposed(uT_of[t], other_of[unit], fe_of[unit], b)

        def transpose_own(t):
            unit, b = divmod(t, BLOCKS)
            pair, i = divmod(unit, STREAMS)
            xT = psum.tile([P, D], F32, tag="xT", bufs=1)
            for j in range(PACK):
                words = maps[pair][i][:, j, b * P : (b + TWO) * P].bitcast(F32)
                nc.tensor.transpose(xT[:, place(j)], words, ident_f32[:])
            xT_of[t] = xT

        def copy_own(t):
            own = work.tile([P, D * TWO], BF16, tag="own", bufs=3)
            words = own[:].bitcast(F32).rearrange("q (w e) -> q w e", e=2)
            nc.scalar.copy(out=words, in_=xT_of[t][:].rearrange("q (e w) -> q w e", e=2))
            own_of[t] = own

        def take_max(t):
            max_r = stats.tile([P, 1], F32, tag="max_r")
            nc.vector.tensor_reduce(out=max_r[:], in_=rT_of[t][:], axis=mybir.AxisListType.X, op=ALU.max)
            max_r_of[t] = max_r

        def exp_max(t):
            max_a = stats.tile([P, 1], F32, tag="max_a")
            nc.scalar.activation(out=max_a[:], in_=max_r_of[t][:], func=ACT.Exp)
            max_a_of[t] = max_a

        def negate(t):
            neg_max = stats.tile([P, 1], F32, tag="neg_max")
            nc.vector.tensor_scalar_mul(out=neg_max[:], in0=max_a_of[t][:], scalar1=-1.0)
            neg_max_of[t] = neg_max

        def first_exp(t):
            e = work.tile([P, D], F32, tag="e", bufs=3)
            nc.scalar.activation(out=e[:], in_=rT_of[t][:], func=ACT.Exp)
            e_of[t] = e

        def second_exp(t):
            sum_e = stats.tile([P, 1], F32, tag="sum_e")
            nc.scalar.activation(out=e_of[t][:], in_=e_of[t][:], func=ACT.Exp, bias=neg_max_of[t][:], accum_out=sum_e[:])
            sum_e_of[t] = sum_e

        def invert_sum(t):
            inv = stats.tile([P, 1], F32, tag="inv")
            nc.vector.reciprocal(out=inv[:], in_=sum_e_of[t][:])
            inv_of[t] = inv

        def weighted_mean(t):
            s = stats.tile([P, 1], F32, tag="s")
            nc.vector.scalar_tensor_tensor(
                out=e_of[t][:],
                in0=e_of[t][:],
                scalar=inv_of[t][:],
                in1=rT_of[t][:],
                op0=ALU.mult,
                op1=ALU.mult,
                accum_out=s[:],
            )
            s_of[t] = s

        def fuse(t):
            k = t % TWO
            coT = work.tile([P, D], BF16, tag="coT", bufs=3)
            nc.vector.scalar_tensor_tensor(
                out=coT[:].rearrange("q (w e) -> q w e", e=2),
                in0=own_of[t - k][:].rearrange("q (w e k) -> q w e k", e=2, k=TWO)[:, :, :, k],
                scalar=s_of[t][:],
                in1=uT_of[t][:].rearrange("q (e w) -> q w e", e=2),
                op0=ALU.mult,
                op1=ALU.add,
            )
            coT_of[t] = coT

        def transpose_back(t):
            k = t % TWO
            if k == 0:
                back = psum.tile([P, 2, TWO * P], F32, tag="back", bufs=1)
                back_of[t] = back
            words = coT_of[t][:].bitcast(F32)
            for u in range(2):
                nc.tensor.transpose(back_of[t - k][:, u, k * P : (k + 1) * P], words[:, u * P : (u + 1) * P], ident_f32[:])

        def group(t):
            unit, b = divmod(t, BLOCKS)
            if b == 0:
                grouped = work.tile([P, HALF * PACK], BF16, tag="grouped", bufs=2, align_bytes=64)
                grouped_of[unit] = grouped
            words = grouped_of[unit][:, b * P * PACK : (b + TWO) * P * PACK].bitcast(F32)
            nc.scalar.copy(out=words.rearrange("p (w u) -> p w u", u=2), in_=back_of[t][:].rearrange("p u w -> p w u"))

        def quantise(unit, first=0, columns=HALF):
            pair, i = divmod(unit, STREAMS)
            if i == 0:
                codes = work.tile([P, STREAMS, HALF], U32, tag="codes", bufs=2, align_bytes=64)
                scales = work.tile([P, STREAMS, HALF], U8, tag="scales", bufs=2, align_bytes=64)
                codes_of[pair], scales_of[pair] = codes, scales
            nc.vector.quantize_mx(
                out=codes_of[pair][:, i, first : first + columns].bitcast(FP8X4),
                scales=scales_of[pair][:, i, first : first + columns],
                in_=grouped_of[unit][:, first * PACK : (first + columns) * PACK],
            )

        def project(pair, k, tag="acc", bufs=1):
            quarter, w, i = k // 4, k // 2 % 2, k % 2
            if k % 4 == 0:
                acc = psum.tile([P, 2, QUARTER], F32, tag=tag, bufs=bufs)
                acc_of[(pair, quarter)] = acc
            q_cols = slice(quarter * QUARTER, (quarter + 1) * QUARTER)
            w_cols = slice((w * STREAMS + i) * OUT, (w * STREAMS + i + 1) * OUT)
            nc.tensor.matmul_mx(
                out=acc_of[(pair, quarter)][:, w, :],
                lhsT=w_codes[:, w_cols].bitcast(FP8X4),
                lhsT_scale=w_scales[:, w_cols],
                rhs=codes_of[pair][:, i, q_cols].bitcast(FP8X4),
                rhs_scale=scales_of[pair][:, i, q_cols],
                start=(i == 0),
                stop=(i == STREAMS - 1),
            )

        def store(pair, quarter):
            n, half = divmod(pair, POS // HALF)
            if quarter == 0:
                result = work.tile([P, 2, HALF], F32, tag="result", bufs=2)
                result_of[pair] = result
            q_cols = slice(quarter * QUARTER, (quarter + 1) * QUARTER)
            for w in range(2):
                nc.scalar.activation(
                    out=result_of[pair][:, w, q_cols].rearrange("p (m e) -> p m e", e=2),
                    in_=acc_of[(pair, quarter)][:, w, :].rearrange("p (e m) -> p m e", e=2),
                    func=ACT.Identity,
                    bias=bias[:, w : w + 1],
                )
            if pair == PAIRS - 1:
                stored = q_cols
            elif quarter == 1:
                stored = slice(0, HALF)
            else:
                return
            for w in range(2):
                nc.sync.dma_start(
                    out=out_views[w][n, :, half * HALF + stored.start : half * HALF + stored.stop],
                    in_=result_of[pair][:, w, stored],
                )

        with tc.manual_schedule():
            for step in range(-8, TILES + 5):
                if step >= 0 and step % 8 == 0 and step // 8 + 2 < PAIRS:
                    load_pair(step // 8 + 2)
                unit = step // BLOCKS + 2
                if unit == 0:
                    if step % BLOCKS == 0:
                        widen(unit)
                        for t in range(2):
                            scale_gate(unit, t, "vector")
                            scale_gate(unit, t + 2, "scalar")
                elif unit < UNITS:
                    if step % BLOCKS == 0:
                        for t in range(3):
                            scale_gate(unit, t, "gpsimd")
                        widen(unit)

                if 0 <= step + 1 < TILES:
                    transpose_r(step + 1)
                if step % 2 == 1 and 0 <= step + 1 < TILES:
                    transpose_own(step + 1)
                if step >= 13 and (step - 13) // 8 < PAIRS - 1:
                    project((step - 13) // 8, (step - 13) % 8)
                if 0 <= step - 1 < TILES:
                    keep_clock(step - 1)
                    transpose_u(step - 1)

                if 0 <= step - 1 < TILES:
                    invert_sum(step - 1)
                if step % 2 == 1 and 0 <= step - 5 < TILES:
                    group(step - 5)
                if step % 2 == 0 and 0 <= step < TILES:
                    copy_own(step)
                if 0 <= step < TILES:
                    exp_max(step)
                    first_exp(step)
                if step % BLOCKS == 2 and 1 <= unit < UNITS:
                    scale_gate(unit, 3, "scalar")
                if 0 <= step - 2 < TILES:
                    fuse(step - 2)
                if 0 <= step < TILES:
                    negate(step)
                if 0 <= step - 3 < TILES:
                    transpose_back(step - 3)
                if step % BLOCKS == 0 and 0 <= step // BLOCKS - 2 < UNITS - 1:
                    quantise(step // BLOCKS - 2)
                if step in (TILES + 2, TILES + 4):
                    quantise(UNITS - 1, (step - TILES - 2) // 2 * QUARTER, QUARTER)
                if 0 <= step - 1 < TILES:
                    weighted_mean(step - 1)
                if 0 <= step + 1 < TILES:
                    take_max(step + 1)
                if 0 <= step < TILES:
                    second_exp(step)
                if step >= 16 and (step - 16) // 8 < PAIRS - 1 and step % 4 == 0:
                    store((step - 16) // 8, step // 4 % 2)
                if step in (TILES + 2, TILES + 4):
                    quarter = (step - TILES - 2) // 2
                    for k in range(4):
                        project(PAIRS - 1, 4 * quarter + k, tag="uT", bufs=2)
                    store(PAIRS - 1, quarter)
